import numpy as np
import ml_dtypes


def mxq(x, axis, fmt="e4m3"):
    dtype, down = {"e4m3": (ml_dtypes.float8_e4m3fn, 7), "e5m2": (ml_dtypes.float8_e5m2, 14)}[fmt]
    v = np.moveaxis(np.asarray(x, np.float32).astype(ml_dtypes.bfloat16).astype(np.float64), axis, -1)
    blocks = v.reshape(v.shape[:-1] + (-1, 32))
    amax = np.abs(blocks).max(-1, keepdims=True)
    byte = np.maximum(np.where(amax > 0, np.frexp(amax)[1] - 1 + 127, 0) - down, 1)
    scale = np.exp2(byte - 127.0)
    codes = (blocks / scale).astype(np.float32).astype(dtype).astype(np.float64)
    return np.moveaxis((codes * scale).reshape(v.shape), -1, axis)


WIDE = False


def mx_kscale(k):
    if not WIDE:
        return np.ones(k)
    levels = np.array([20, -20, 10, -10, 0])
    a = np.random.permutation(np.resize(levels, k // 512 * 4)).reshape(k // 512, 4)
    idx = np.arange(k)
    return np.exp2(a[idx // 512, idx % 128 // 32])


BF16 = ml_dtypes.bfloat16


def bf(x):
    return np.asarray(x, np.float32).astype(BF16)


def f64(x):
    return np.asarray(x).astype(np.float64)


B, A, E, P, R = 512, 8, 512, 512, 512


def setup_inputs():
    u = mx_kscale(P)
    attr_rep = bf(np.random.standard_normal((B, A, R)))
    w0 = bf(np.random.standard_normal((A, R, P)) / np.sqrt(R))
    self_weighted = bf(1.0 + 0.3 * np.random.standard_normal((1, A, 1)))
    g = bf(np.random.standard_normal((B, P)) * np.exp2(np.random.randint(-12, 1, (B, 1))) * 16.0 * u)
    proj = (f64(attr_rep).transpose(1, 0, 2) @ f64(w0)).transpose(1, 0, 2)
    return {
        "attr_rep": attr_rep,
        "bwd_proj": bf(f64(w0) / u),
        "self_weighted": self_weighted,
        "proj": np.asarray(proj, np.float32),
        "grad_out": g,
    }


def reference(attr_rep, bwd_proj, self_weighted, proj, grad_out):
    mask = np.where(f64(proj) > 0.0, 1.0, 0.0)
    dz = f64(grad_out)[:, None, :] * f64(self_weighted) * mask
    dzq = mxq(dz.transpose(1, 0, 2), 2, "e5m2")
    wq = mxq(f64(bwd_proj), 2, "e4m3")
    return (dzq @ wq.transpose(0, 2, 1)).transpose(1, 0, 2)

@@ -1,0 +1,182 @@
+from contextlib import ExitStack
+
+import concourse.mybir as mybir
+from concourse.masks import make_identity
+
+F32 = mybir.dt.float32
+BF16 = mybir.dt.bfloat16
+U32 = mybir.dt.uint32
+U8 = mybir.dt.uint8
+E4M3_X4 = mybir.dt.float8_e4m3fn_x4
+E5M2_X4 = mybir.dt.float8_e5m2_x4
+ALU = mybir.AluOpType
+
+P = 128
+NODES = 512
+TYPES = 8
+K = 512
+ROWS = 512
+PACK = 4
+STRIDE = NODES // P
+HALF_TYPES = TYPES // 2
+CHUNKS = STRIDE * 2
+K_WORDS = K // 2
+
+FLOPS = 2 * NODES * TYPES * K * ROWS
+BYTES = NODES * TYPES * K * 4 + TYPES * ROWS * K * 2 + NODES * K * 2 + TYPES * 2 + NODES * TYPES * ROWS * 4
+
+
+def tile_attributegnn_pb_v_kernel(tc, attr_rep, bwd_proj, self_weighted, proj, grad_out, out):
+    nc = tc.nc
+    proj_view = proj.rearrange("(q j) a k -> q j a k", j=STRIDE)
+    out_view = out.rearrange("(q j) a r -> q j a r", j=STRIDE)
+
+    with ExitStack() as ctx:
+        keep = ctx.enter_context(tc.tile_pool(name="keep", bufs=1))
+        w_in = ctx.enter_context(tc.tile_pool(name="w_in", bufs=TYPES // 2))
+        proj_in = ctx.enter_context(tc.tile_pool(name="proj_in", bufs=CHUNKS))
+        work = ctx.enter_context(tc.tile_pool(name="work", bufs=3))
+        out_pool = ctx.enter_context(tc.tile_pool(name="out_pool", bufs=6))
+        psum_w = ctx.enter_context(tc.psum_pool(name="psum_w", bufs=2))
+        psum_dz = ctx.enter_context(tc.psum_pool(name="psum_dz", bufs=4))
+        psum_mx = ctx.enter_context(tc.psum_pool(name="psum_mx", bufs=2))
+
+        g_raw = keep.tile([P, STRIDE, K], BF16)
+        nc.sync.dma_start(out=g_raw[:], in_=grad_out.rearrange("(q j) k -> q j k", j=STRIDE))
+        sw_bf16 = keep.tile([P, TYPES], BF16)
+        nc.scalar.dma_start(
+            out=sw_bf16[:], in_=self_weighted.rearrange("o a i -> (o a i)").partition_broadcast(P)
+        )
+
+        def load_proj(c):
+            chunk = proj_in.tile([P, HALF_TYPES, K], F32, name="proj_chunk")
+            first = (c // STRIDE) * HALF_TYPES
+            nc.sync.dma_start(out=chunk[:], in_=proj_view[:, c % STRIDE, first : first + HALF_TYPES, :])
+            return chunk
+
+        def load_w_pair(pair):
+            raw = w_in.tile([P, 2, STRIDE * K], BF16, name="w_raw")
+            nc.sync.dma_start(
+                out=raw[:],
+                in_=bwd_proj[2 * pair : 2 * pair + 2].rearrange("a (q j) k -> q a (j k)", j=STRIDE),
+            )
+            return raw
+
+        proj_chunks = [load_proj(0)]
+        w_raws = [load_w_pair(0), load_w_pair(1)]
+        proj_chunks.extend([load_proj(c) for c in range(1, STRIDE)])
+        w_raws.extend([load_w_pair(2), load_w_pair(3)])
+        proj_chunks.extend([load_proj(c) for c in range(STRIDE, CHUNKS)])
+
+        ident = keep.tile([P, P], F32)
+        make_identity(nc, ident[:])
+        sw = keep.tile([P, TYPES], F32)
+        nc.vector.tensor_copy(out=sw[:], in_=sw_bf16[:])
+
+        g_t = keep.tile([P, STRIDE, 2 * P * PACK], BF16)
+        g_words = g_raw[:].bitcast(F32)
+        g_t_words = g_t[:].bitcast(F32).rearrange("p j (d q u) -> p j d q u", d=2, u=2)
+        for jp in range(STRIDE // 2):
+            g_bank = psum_dz.tile([P, 2, 2, P], F32, tag="dz_bank", name="g_bank")
+            for jj in range(2):
+                for u in range(2):
+                    nc.tensor.transpose(
+                        g_bank[:, u, jj, :], g_words[:, 2 * jp + jj, u * P : (u + 1) * P], ident[:]
+                    )
+            for d in range(2):
+                nc.vector.tensor_copy(
+                    out=g_t_words[:, 2 * jp : 2 * jp + 2, d, :, :],
+                    in_=g_bank[:].rearrange("p u jj q -> p jj q u"),
+                )
+
+        w_codes = keep.tile([P, TYPES, ROWS], U32, align_bytes=64)
+        w_scales = keep.tile([P, TYPES, ROWS], U8, align_bytes=64)
+
+        def prepare_weights(a):
+            w_words = w_raws[a // 2][:].bitcast(F32)
+            w_grouped = work.tile([P, ROWS * PACK], BF16, align_bytes=64, name="w_grouped")
+            grouped_words = w_grouped[:].bitcast(F32).rearrange("p (q h s) -> p q h s", h=2, s=4)
+            for h in range(2):
+                w_bank = psum_w.tile([P, 4, P], F32, name="w_bank")
+                for jj in range(2):
+                    for u in range(2):
+                        start = (2 * h + jj) * K_WORDS + u * P
+                        nc.tensor.transpose(
+                            w_bank[:, 2 * jj + u, :], w_words[:, a % 2, start : start + P], ident[:]
+                        )
+                nc.scalar.copy(out=grouped_words[:, :, h, :], in_=w_bank[:].rearrange("p s q -> p q s"))
+            nc.vector.quantize_mx(
+                out=w_codes[:, a, :].bitcast(E4M3_X4), scales=w_scales[:, a, :], in_=w_grouped[:]
+            )
+
+        def mask_and_transpose(c):
+            first = (c // STRIDE) * HALF_TYPES
+            masked_sw = work.tile([P, HALF_TYPES, K], BF16, name="masked_sw")
+            for al in range(HALF_TYPES):
+                nc.vector.tensor_scalar(
+                    out=masked_sw[:, al, :],
+                    in0=proj_chunks[c][:, al, :],
+                    scalar1=0.0,
+                    scalar2=sw[:, first + al : first + al + 1],
+                    op0=ALU.is_gt,
+                    op1=ALU.mult,
+                )
+            mask_words = masked_sw[:].bitcast(F32)
+            banks = []
+            for pair in range(HALF_TYPES // 2):
+                dz_bank = psum_dz.tile([P, 2, 2, P], F32, tag="dz_bank", name="dz_bank")
+                for a2 in range(2):
+                    for u in range(2):
+                        nc.tensor.transpose(
+                            dz_bank[:, u, a2, :], mask_words[:, 2 * pair + a2, u * P : (u + 1) * P], ident[:]
+                        )
+                banks.append(dz_bank)
+            return banks
+
+        def multiply_and_quantise(c, banks):
+            dz_grouped = work.tile([P, HALF_TYPES * P * PACK], BF16, align_bytes=64, name="dz_grouped")
+            width = 2 * P * PACK
+            for pair in range(HALF_TYPES // 2):
+                nc.vector.tensor_tensor(
+                    out=dz_grouped[:, pair * width : (pair + 1) * width].rearrange(
+                        "p (c u e) -> p c u e", u=2, e=2
+                    ),
+                    in0=banks[pair][:]
+                    .rearrange("p u a q -> p u (a q)")
+                    .bitcast(BF16)
+                    .rearrange("p u (c e) -> p c u e", e=2),
+                    in1=g_t[:, c % STRIDE, :].rearrange("p (c u e) -> p c u e", u=2, e=2),
+                    op=ALU.mult,
+                )
+            dz_codes = work.tile([P, HALF_TYPES * P], U32, align_bytes=64, name="dz_codes")
+            dz_scales = work.tile([P, HALF_TYPES * P], U8, align_bytes=64, name="dz_scales")
+            nc.vector.quantize_mx(out=dz_codes[:].bitcast(E5M2_X4), scales=dz_scales[:], in_=dz_grouped[:])
+            return dz_codes, dz_scales
+
+        def matmul_and_store(c, dz_codes, dz_scales):
+            first = (c // STRIDE) * HALF_TYPES
+            result = out_pool.tile([P, HALF_TYPES, ROWS], F32, name="result")
+            for al in range(HALF_TYPES):
+                acc = psum_mx.tile([P, ROWS], F32, name="acc")
+                nc.tensor.matmul_mx(
+                    out=acc[:],
+                    lhsT=dz_codes[:, al * P : (al + 1) * P].bitcast(E5M2_X4),
+                    lhsT_scale=dz_scales[:, al * P : (al + 1) * P],
+                    rhs=w_codes[:, first + al, :].bitcast(E4M3_X4),
+                    rhs_scale=w_scales[:, first + al, :],
+                    start=True,
+                    stop=True,
+                )
+                nc.scalar.copy(out=result[:, al, :], in_=acc[:])
+            nc.sync.dma_start(out=out_view[:, c % STRIDE, first : first + HALF_TYPES, :], in_=result[:])
+
+        banks_of = {}
+        for c in range(CHUNKS + 1):
+            if c < CHUNKS:
+                banks_of[c] = mask_and_transpose(c)
+                if c % STRIDE == 0:
+                    for a in range((c // STRIDE) * HALF_TYPES, (c // STRIDE + 1) * HALF_TYPES):
+                        prepare_weights(a)
+            if c >= 1:
+                dz_codes, dz_scales = multiply_and_quantise(c - 1, banks_of[c - 1])
+                matmul_and_store(c - 1, dz_codes, dz_scales)

@@ -62,11 +62,12 @@ def tile_attributegnn_pb_v_kernel(tc, attr_rep, bwd_proj, self_weighted, proj, g
             )
             return raw
 
-        proj_chunks = [load_proj(0)]
-        w_raws = [load_w_pair(0), load_w_pair(1)]
-        proj_chunks.extend([load_proj(c) for c in range(1, STRIDE)])
-        w_raws.extend([load_w_pair(2), load_w_pair(3)])
-        proj_chunks.extend([load_proj(c) for c in range(STRIDE, CHUNKS)])
+        proj_chunks = []
+        w_raws = []
+        for c in range(CHUNKS):
+            proj_chunks.append(load_proj(c))
+            if c < TYPES // 2:
+                w_raws.append(load_w_pair(c))
 
         ident = keep.tile([P, P], F32)
         make_identity(nc, ident[:])
@@ -174,9 +175,9 @@ def tile_attributegnn_pb_v_kernel(tc, attr_rep, bwd_proj, self_weighted, proj, g
         for c in range(CHUNKS + 1):
             if c < CHUNKS:
                 banks_of[c] = mask_and_transpose(c)
-                if c % STRIDE == 0:
-                    for a in range((c // STRIDE) * HALF_TYPES, (c // STRIDE + 1) * HALF_TYPES):
-                        prepare_weights(a)
+                if c < TYPES // 2:
+                    prepare_weights(2 * c)
+                    prepare_weights(2 * c + 1)
             if c >= 1:
                 dz_codes, dz_scales = multiply_and_quantise(c - 1, banks_of[c - 1])
                 matmul_and_store(c - 1, dz_codes, dz_scales)

@@ -38,8 +38,8 @@ def tile_attributegnn_pb_v_kernel(tc, attr_rep, bwd_proj, self_weighted, proj, g
         work = ctx.enter_context(tc.tile_pool(name="work", bufs=3))
         out_pool = ctx.enter_context(tc.tile_pool(name="out_pool", bufs=6))
         psum_w = ctx.enter_context(tc.psum_pool(name="psum_w", bufs=2))
-        psum_dz = ctx.enter_context(tc.psum_pool(name="psum_dz", bufs=4))
-        psum_mx = ctx.enter_context(tc.psum_pool(name="psum_mx", bufs=2))
+        psum_dz = ctx.enter_context(tc.psum_pool(name="psum_dz", bufs=3))
+        psum_mx = ctx.enter_context(tc.psum_pool(name="psum_mx", bufs=3))
 
         g_raw = keep.tile([P, STRIDE, K], BF16)
         nc.sync.dma_start(out=g_raw[:], in_=grad_out.rearrange("(q j) k -> q j k", j=STRIDE))

@@ -43,10 +43,11 @@ def tile_attributegnn_pb_v_kernel(tc, attr_rep, bwd_proj, self_weighted, proj, g
 
         g_raw = keep.tile([P, STRIDE, K], BF16)
         nc.sync.dma_start(out=g_raw[:], in_=grad_out.rearrange("(q j) k -> q j k", j=STRIDE))
-        sw_bf16 = keep.tile([P, TYPES], BF16)
-        nc.scalar.dma_start(
-            out=sw_bf16[:], in_=self_weighted.rearrange("o a i -> (o a i)").partition_broadcast(P)
-        )
+        sw_row = keep.tile([P, TYPES], BF16)
+        nc.vector.memset(sw_row[:], 0.0)
+        nc.scalar.dma_start(out=sw_row[0:1, :], in_=self_weighted.rearrange("o a i -> o (a i)"))
+        ones = keep.tile([P, P], BF16)
+        nc.vector.memset(ones[:], 1.0)
 
         def load_proj(c):
             chunk = proj_in.tile([P, HALF_TYPES, K], F32, name="proj_chunk")
@@ -72,7 +73,9 @@ def tile_attributegnn_pb_v_kernel(tc, attr_rep, bwd_proj, self_weighted, proj, g
         ident = keep.tile([P, P], F32)
         make_identity(nc, ident[:])
         sw = keep.tile([P, TYPES], F32)
-        nc.vector.tensor_copy(out=sw[:], in_=sw_bf16[:])
+        sw_bank = psum_w.tile([P, TYPES], F32, tag="w_bank", name="sw_bank")
+        nc.tensor.matmul(sw_bank[:], lhsT=ones[:], rhs=sw_row[:], start=True, stop=True)
+        nc.vector.tensor_copy(out=sw[:], in_=sw_bank[:])
 
         g_t = keep.tile([P, STRIDE, 2 * P * PACK], BF16)
         g_words = g_raw[:].bitcast(F32)
@@ -98,7 +101,7 @@ def tile_attributegnn_pb_v_kernel(tc, attr_rep, bwd_proj, self_weighted, proj, g
             w_grouped = work.tile([P, ROWS * PACK], BF16, align_bytes=64, name="w_grouped")
             grouped_words = w_grouped[:].bitcast(F32).rearrange("p (q h s) -> p q h s", h=2, s=4)
             for h in range(2):
-                w_bank = psum_w.tile([P, 4, P], F32, name="w_bank")
+                w_bank = psum_w.tile([P, 4, P], F32, tag="w_bank", name="w_bank")
                 for jj in range(2):
                     for u in range(2):
                         start = (2 * h + jj) * K_WORDS + u * P

@@ -45,7 +45,7 @@ def tile_attributegnn_pb_v_kernel(tc, attr_rep, bwd_proj, self_weighted, proj, g
         nc.sync.dma_start(out=g_raw[:], in_=grad_out.rearrange("(q j) k -> q j k", j=STRIDE))
         sw_row = keep.tile([P, TYPES], BF16)
         nc.vector.memset(sw_row[:], 0.0)
-        nc.scalar.dma_start(out=sw_row[0:1, :], in_=self_weighted.rearrange("o a i -> o (a i)"))
+        nc.sync.dma_start(out=sw_row[0:1, :], in_=self_weighted.rearrange("o a i -> o (a i)"))
         ones = keep.tile([P, P], BF16)
         nc.vector.memset(ones[:], 1.0)
 
@@ -77,9 +77,9 @@ def tile_attributegnn_pb_v_kernel(tc, attr_rep, bwd_proj, self_weighted, proj, g
         nc.tensor.matmul(sw_bank[:], lhsT=ones[:], rhs=sw_row[:], start=True, stop=True)
         nc.vector.tensor_copy(out=sw[:], in_=sw_bank[:])
 
-        g_t = keep.tile([P, STRIDE, 2 * P * PACK], BF16)
+        g_t = keep.tile([P, STRIDE, 1, P * PACK], BF16)
         g_words = g_raw[:].bitcast(F32)
-        g_t_words = g_t[:].bitcast(F32).rearrange("p j (d q u) -> p j d q u", d=2, u=2)
+        g_t_words = g_t[:].bitcast(F32).rearrange("p j o (q u) -> p (j o) q u", u=2)
         for jp in range(STRIDE // 2):
             g_bank = psum_dz.tile([P, 2, 2, P], F32, tag="dz_bank", name="g_bank")
             for jj in range(2):
@@ -87,11 +87,10 @@ def tile_attributegnn_pb_v_kernel(tc, attr_rep, bwd_proj, self_weighted, proj, g
                     nc.tensor.transpose(
                         g_bank[:, u, jj, :], g_words[:, 2 * jp + jj, u * P : (u + 1) * P], ident[:]
                     )
-            for d in range(2):
-                nc.vector.tensor_copy(
-                    out=g_t_words[:, 2 * jp : 2 * jp + 2, d, :, :],
-                    in_=g_bank[:].rearrange("p u jj q -> p jj q u"),
-                )
+            nc.vector.tensor_copy(
+                out=g_t_words[:, 2 * jp : 2 * jp + 2, :, :],
+                in_=g_bank[:].rearrange("p u jj q -> p jj q u"),
+            )
 
         w_codes = keep.tile([P, TYPES, ROWS], U32, align_bytes=64)
         w_scales = keep.tile([P, TYPES, ROWS], U8, align_bytes=64)
@@ -140,16 +139,17 @@ def tile_attributegnn_pb_v_kernel(tc, attr_rep, bwd_proj, self_weighted, proj, g
         def multiply_and_quantise(c, banks):
             dz_grouped = work.tile([P, HALF_TYPES * P * PACK], BF16, align_bytes=64, name="dz_grouped")
             width = 2 * P * PACK
+            g_pair = g_t[:, c % STRIDE, :, :].to_broadcast([P, 2, P * PACK])
             for pair in range(HALF_TYPES // 2):
                 nc.vector.tensor_tensor(
                     out=dz_grouped[:, pair * width : (pair + 1) * width].rearrange(
-                        "p (c u e) -> p c u e", u=2, e=2
+                        "p (a q u e) -> p a q u e", a=2, u=2, e=2
                     ),
                     in0=banks[pair][:]
                     .rearrange("p u a q -> p u (a q)")
                     .bitcast(BF16)
-                    .rearrange("p u (c e) -> p c u e", e=2),
-                    in1=g_t[:, c % STRIDE, :].rearrange("p (c u e) -> p c u e", u=2, e=2),
+                    .rearrange("p u (a q e) -> p a q u e", a=2, e=2),
+                    in1=g_pair.rearrange("p a (q u e) -> p a q u e", u=2, e=2),
                     op=ALU.mult,
                 )
             dz_codes = work.tile([P, HALF_TYPES * P], U32, align_bytes=64, name="dz_codes")

@@ -171,7 +171,10 @@ def tile_attributegnn_pb_v_kernel(tc, attr_rep, bwd_proj, self_weighted, proj, g
                     start=True,
                     stop=True,
                 )
-                nc.scalar.copy(out=result[:, al, :], in_=acc[:])
+                if c >= CHUNKS - 2 and al == HALF_TYPES - 1:
+                    nc.vector.tensor_copy(out=result[:, al, :], in_=acc[:])
+                else:
+                    nc.scalar.copy(out=result[:, al, :], in_=acc[:])
             nc.sync.dma_start(out=out_view[:, c % STRIDE, first : first + HALF_TYPES, :], in_=result[:])
 
         banks_of = {}

@@ -21,6 +21,7 @@ STRIDE = NODES // P
 HALF_TYPES = TYPES // 2
 CHUNKS = STRIDE * 2
 K_WORDS = K // 2
+W_LOW = 2 * ROWS // P
 
 FLOPS = 2 * NODES * TYPES * K * ROWS
 BYTES = NODES * TYPES * K * 4 + TYPES * ROWS * K * 2 + NODES * K * 2 + TYPES * 2 + NODES * TYPES * ROWS * 4
@@ -36,7 +37,7 @@ def tile_attributegnn_pb_v_kernel(tc, attr_rep, bwd_proj, self_weighted, proj, g
         w_in = ctx.enter_context(tc.tile_pool(name="w_in", bufs=TYPES // 2))
         proj_in = ctx.enter_context(tc.tile_pool(name="proj_in", bufs=CHUNKS))
         work = ctx.enter_context(tc.tile_pool(name="work", bufs=3))
-        out_pool = ctx.enter_context(tc.tile_pool(name="out_pool", bufs=6))
+        out_pool = ctx.enter_context(tc.tile_pool(name="out_pool", bufs=5))
         psum_w = ctx.enter_context(tc.psum_pool(name="psum_w", bufs=2))
         psum_dz = ctx.enter_context(tc.psum_pool(name="psum_dz", bufs=3))
         psum_mx = ctx.enter_context(tc.psum_pool(name="psum_mx", bufs=3))
@@ -56,10 +57,10 @@ def tile_attributegnn_pb_v_kernel(tc, attr_rep, bwd_proj, self_weighted, proj, g
             return chunk
 
         def load_w_pair(pair):
-            raw = w_in.tile([P, 2, STRIDE * K], BF16, name="w_raw")
+            raw = w_in.tile([P, W_LOW * K], BF16, name="w_raw")
             nc.sync.dma_start(
                 out=raw[:],
-                in_=bwd_proj[2 * pair : 2 * pair + 2].rearrange("a (q j) k -> q a (j k)", j=STRIDE),
+                in_=bwd_proj[2 * pair : 2 * pair + 2].rearrange("a (h l) k -> (a h) (l k)", l=W_LOW),
             )
             return raw
 
@@ -95,22 +96,25 @@ def tile_attributegnn_pb_v_kernel(tc, attr_rep, bwd_proj, self_weighted, proj, g
         w_codes = keep.tile([P, TYPES, ROWS], U32, align_bytes=64)
         w_scales = keep.tile([P, TYPES, ROWS], U8, align_bytes=64)
 
-        def prepare_weights(a):
-            w_words = w_raws[a // 2][:].bitcast(F32)
-            w_grouped = work.tile([P, ROWS * PACK], BF16, align_bytes=64, name="w_grouped")
-            grouped_words = w_grouped[:].bitcast(F32).rearrange("p (q h s) -> p q h s", h=2, s=4)
-            for h in range(2):
-                w_bank = psum_w.tile([P, 4, P], F32, tag="w_bank", name="w_bank")
-                for jj in range(2):
+        def prepare_weights(pair):
+            w_words = w_raws[pair][:].bitcast(F32)
+            w_grouped = work.tile([P, 2, ROWS * PACK], BF16, align_bytes=64, name="w_grouped")
+            grouped_words = w_grouped[:].bitcast(F32).rearrange("p a (l h u) -> p a l h u", l=W_LOW, u=2)
+            for lp in range(W_LOW // 2):
+                w_bank = psum_w.tile([P, 2, 2, P], F32, tag="w_bank", name="w_bank")
+                for ll in range(2):
                     for u in range(2):
-                        start = (2 * h + jj) * K_WORDS + u * P
-                        nc.tensor.transpose(
-                            w_bank[:, 2 * jj + u, :], w_words[:, a % 2, start : start + P], ident[:]
-                        )
-                nc.scalar.copy(out=grouped_words[:, :, h, :], in_=w_bank[:].rearrange("p s q -> p q s"))
-            nc.vector.quantize_mx(
-                out=w_codes[:, a, :].bitcast(E4M3_X4), scales=w_scales[:, a, :], in_=w_grouped[:]
-            )
+                        start = (2 * lp + ll) * K_WORDS + u * P
+                        nc.tensor.transpose(w_bank[:, ll, u, :], w_words[:, start : start + P], ident[:])
+                nc.scalar.copy(
+                    out=grouped_words[:, :, 2 * lp : 2 * lp + 2, :, :],
+                    in_=w_bank[:].rearrange("p l u (a h) -> p a l h u", a=2),
+                )
+            for i in range(2):
+                a = 2 * pair + i
+                nc.vector.quantize_mx(
+                    out=w_codes[:, a, :].bitcast(E4M3_X4), scales=w_scales[:, a, :], in_=w_grouped[:, i, :]
+                )
 
         def mask_and_transpose(c):
             first = (c // STRIDE) * HALF_TYPES
@@ -171,10 +175,12 @@ def tile_attributegnn_pb_v_kernel(tc, attr_rep, bwd_proj, self_weighted, proj, g
                     start=True,
                     stop=True,
                 )
+                rows_out = result[:, al, :].rearrange("q (h l) -> q h l", l=W_LOW)
+                rows_in = acc[:].rearrange("q (l h) -> q h l", l=W_LOW)
                 if c >= CHUNKS - 2 and al == HALF_TYPES - 1:
-                    nc.vector.tensor_copy(out=result[:, al, :], in_=acc[:])
+                    nc.vector.tensor_copy(out=rows_out, in_=rows_in)
                 else:
-                    nc.scalar.copy(out=result[:, al, :], in_=acc[:])
+                    nc.scalar.copy(out=rows_out, in_=rows_in)
             nc.sync.dma_start(out=out_view[:, c % STRIDE, first : first + HALF_TYPES, :], in_=result[:])
 
         banks_of = {}
@@ -182,8 +188,7 @@ def tile_attributegnn_pb_v_kernel(tc, attr_rep, bwd_proj, self_weighted, proj, g
             if c < CHUNKS:
                 banks_of[c] = mask_and_transpose(c)
                 if c < TYPES // 2:
-                    prepare_weights(2 * c)
-                    prepare_weights(2 * c + 1)
+                    prepare_weights(c)
             if c >= 1:
                 dz_codes, dz_scales = multiply_and_quantise(c - 1, banks_of[c - 1])
                 matmul_and_store(c - 1, dz_codes, dz_scales)

@@ -177,11 +177,18 @@ def tile_attributegnn_pb_v_kernel(tc, attr_rep, bwd_proj, self_weighted, proj, g
                 )
                 rows_out = result[:, al, :].rearrange("q (h l) -> q h l", l=W_LOW)
                 rows_in = acc[:].rearrange("q (l h) -> q h l", l=W_LOW)
-                if c >= CHUNKS - 2 and al == HALF_TYPES - 1:
+                if c == CHUNKS - 1 and al % 2 == 1:
                     nc.vector.tensor_copy(out=rows_out, in_=rows_in)
                 else:
                     nc.scalar.copy(out=rows_out, in_=rows_in)
-            nc.sync.dma_start(out=out_view[:, c % STRIDE, first : first + HALF_TYPES, :], in_=result[:])
+                if c == CHUNKS - 1 and al % 2 == 1:
+                    queue = nc.sync if al == 1 else nc.scalar
+                    queue.dma_start(
+                        out=out_view[:, c % STRIDE, first + al - 1 : first + al + 1, :], in_=result[:, al - 1 : al + 1, :]
+                    )
+            if c < CHUNKS - 1:
+                queue = nc.scalar if c in (4, 6) else nc.sync
+                queue.dma_start(out=out_view[:, c % STRIDE, first : first + HALF_TYPES, :], in_=result[:])
 
         banks_of = {}
         for c in range(CHUNKS + 1):

@@ -29,8 +29,8 @@ BYTES = NODES * TYPES * K * 4 + TYPES * ROWS * K * 2 + NODES * K * 2 + TYPES * 2
 
 def tile_attributegnn_pb_v_kernel(tc, attr_rep, bwd_proj, self_weighted, proj, grad_out, out):
     nc = tc.nc
-    proj_view = proj.rearrange("(q j) a k -> q j a k", j=STRIDE)
-    out_view = out.rearrange("(q j) a r -> q j a r", j=STRIDE)
+    proj_view = proj.rearrange("(j q) a k -> q j a k", j=STRIDE)
+    out_view = out.rearrange("(j q) a r -> q j a r", j=STRIDE)
 
     with ExitStack() as ctx:
         keep = ctx.enter_context(tc.tile_pool(name="keep", bufs=1))
@@ -43,7 +43,7 @@ def tile_attributegnn_pb_v_kernel(tc, attr_rep, bwd_proj, self_weighted, proj, g
         psum_mx = ctx.enter_context(tc.psum_pool(name="psum_mx", bufs=3))
 
         g_raw = keep.tile([P, STRIDE, K], BF16)
-        nc.sync.dma_start(out=g_raw[:], in_=grad_out.rearrange("(q j) k -> q j k", j=STRIDE))
+        nc.sync.dma_start(out=g_raw[:], in_=grad_out.rearrange("(j q) k -> q j k", j=STRIDE))
         sw_row = keep.tile([P, TYPES], BF16)
         nc.vector.memset(sw_row[:], 0.0)
         nc.sync.dma_start(out=sw_row[0:1, :], in_=self_weighted.rearrange("o a i -> o (a i)"))

from contextlib import ExitStack

import concourse.mybir as mybir
from concourse.masks import make_identity

F32 = mybir.dt.float32
BF16 = mybir.dt.bfloat16
U32 = mybir.dt.uint32
U8 = mybir.dt.uint8
E4M3_X4 = mybir.dt.float8_e4m3fn_x4
E5M2_X4 = mybir.dt.float8_e5m2_x4
ALU = mybir.AluOpType

P = 128
NODES = 512
TYPES = 8
K = 512
ROWS = 512
PACK = 4
STRIDE = NODES // P
HALF_TYPES = TYPES // 2
CHUNKS = STRIDE * 2
K_WORDS = K // 2
W_LOW = 2 * ROWS // P

FLOPS = 2 * NODES * TYPES * K * ROWS
BYTES = NODES * TYPES * K * 4 + TYPES * ROWS * K * 2 + NODES * K * 2 + TYPES * 2 + NODES * TYPES * ROWS * 4


def tile_attributegnn_pb_v_kernel(tc, attr_rep, bwd_proj, self_weighted, proj, grad_out, out):
    nc = tc.nc
    proj_view = proj.rearrange("(j q) a k -> q j a k", j=STRIDE)
    out_view = out.rearrange("(j q) a r -> q j a r", j=STRIDE)

    with ExitStack() as ctx:
        keep = ctx.enter_context(tc.tile_pool(name="keep", bufs=1))
        w_in = ctx.enter_context(tc.tile_pool(name="w_in", bufs=TYPES // 2))
        proj_in = ctx.enter_context(tc.tile_pool(name="proj_in", bufs=CHUNKS))
        work = ctx.enter_context(tc.tile_pool(name="work", bufs=3))
        out_pool = ctx.enter_context(tc.tile_pool(name="out_pool", bufs=5))
        psum_w = ctx.enter_context(tc.psum_pool(name="psum_w", bufs=2))
        psum_dz = ctx.enter_context(tc.psum_pool(name="psum_dz", bufs=3))
        psum_mx = ctx.enter_context(tc.psum_pool(name="psum_mx", bufs=3))

        g_raw = keep.tile([P, STRIDE, K], BF16)
        nc.sync.dma_start(out=g_raw[:], in_=grad_out.rearrange("(j q) k -> q j k", j=STRIDE))
        sw_row = keep.tile([P, TYPES], BF16)
        nc.vector.memset(sw_row[:], 0.0)
        nc.sync.dma_start(out=sw_row[0:1, :], in_=self_weighted.rearrange("o a i -> o (a i)"))
        ones = keep.tile([P, P], BF16)
        nc.vector.memset(ones[:], 1.0)

        def load_proj(c):
            chunk = proj_in.tile([P, HALF_TYPES, K], F32, name="proj_chunk")
            first = (c // STRIDE) * HALF_TYPES
            nc.sync.dma_start(out=chunk[:], in_=proj_view[:, c % STRIDE, first : first + HALF_TYPES, :])
            return chunk

        def load_w_pair(pair):
            raw = w_in.tile([P, W_LOW * K], BF16, name="w_raw")
            nc.sync.dma_start(
                out=raw[:],
                in_=bwd_proj[2 * pair : 2 * pair + 2].rearrange("a (h l) k -> (a h) (l k)", l=W_LOW),
            )
            return raw

        proj_chunks = []
        w_raws = []
        for c in range(CHUNKS):
            proj_chunks.append(load_proj(c))
            if c < TYPES // 2:
                w_raws.append(load_w_pair(c))

        ident = keep.tile([P, P], F32)
        make_identity(nc, ident[:])
        sw = keep.tile([P, TYPES], F32)
        sw_bank = psum_w.tile([P, TYPES], F32, tag="w_bank", name="sw_bank")
        nc.tensor.matmul(sw_bank[:], lhsT=ones[:], rhs=sw_row[:], start=True, stop=True)
        nc.vector.tensor_copy(out=sw[:], in_=sw_bank[:])

        g_t = keep.tile([P, STRIDE, 1, P * PACK], BF16)
        g_words = g_raw[:].bitcast(F32)
        g_t_words = g_t[:].bitcast(F32).rearrange("p j o (q u) -> p (j o) q u", u=2)
        for jp in range(STRIDE // 2):
            g_bank = psum_dz.tile([P, 2, 2, P], F32, tag="dz_bank", name="g_bank")
            for jj in range(2):
                for u in range(2):
                    nc.tensor.transpose(
                        g_bank[:, u, jj, :], g_words[:, 2 * jp + jj, u * P : (u + 1) * P], ident[:]
                    )
            nc.vector.tensor_copy(
                out=g_t_words[:, 2 * jp : 2 * jp + 2, :, :],
                in_=g_bank[:].rearrange("p u jj q -> p jj q u"),
            )

        w_codes = keep.tile([P, TYPES, ROWS], U32, align_bytes=64)
        w_scales = keep.tile([P, TYPES, ROWS], U8, align_bytes=64)

        def prepare_weights(pair):
            w_words = w_raws[pair][:].bitcast(F32)
            w_grouped = work.tile([P, 2, ROWS * PACK], BF16, align_bytes=64, name="w_grouped")
            grouped_words = w_grouped[:].bitcast(F32).rearrange("p a (l h u) -> p a l h u", l=W_LOW, u=2)
            for lp in range(W_LOW // 2):
                w_bank = psum_w.tile([P, 2, 2, P], F32, tag="w_bank", name="w_bank")
                for ll in range(2):
                    for u in range(2):
                        start = (2 * lp + ll) * K_WORDS + u * P
                        nc.tensor.transpose(w_bank[:, ll, u, :], w_words[:, start : start + P], ident[:])
                nc.scalar.copy(
                    out=grouped_words[:, :, 2 * lp : 2 * lp + 2, :, :],
                    in_=w_bank[:].rearrange("p l u (a h) -> p a l h u", a=2),
                )
            for i in range(2):
                a = 2 * pair + i
                nc.vector.quantize_mx(
                    out=w_codes[:, a, :].bitcast(E4M3_X4), scales=w_scales[:, a, :], in_=w_grouped[:, i, :]
                )

        def mask_and_transpose(c):
            first = (c // STRIDE) * HALF_TYPES
            masked_sw = work.tile([P, HALF_TYPES, K], BF16, name="masked_sw")
            for al in range(HALF_TYPES):
                nc.vector.tensor_scalar(
                    out=masked_sw[:, al, :],
                    in0=proj_chunks[c][:, al, :],
                    scalar1=0.0,
                    scalar2=sw[:, first + al : first + al + 1],
                    op0=ALU.is_gt,
                    op1=ALU.mult,
                )
            mask_words = masked_sw[:].bitcast(F32)
            banks = []
            for pair in range(HALF_TYPES // 2):
                dz_bank = psum_dz.tile([P, 2, 2, P], F32, tag="dz_bank", name="dz_bank")
                for a2 in range(2):
                    for u in range(2):
                        nc.tensor.transpose(
                            dz_bank[:, u, a2, :], mask_words[:, 2 * pair + a2, u * P : (u + 1) * P], ident[:]
                        )
                banks.append(dz_bank)
            return banks

        def multiply_and_quantise(c, banks):
            dz_grouped = work.tile([P, HALF_TYPES * P * PACK], BF16, align_bytes=64, name="dz_grouped")
            width = 2 * P * PACK
            g_pair = g_t[:, c % STRIDE, :, :].to_broadcast([P, 2, P * PACK])
            for pair in range(HALF_TYPES // 2):
                nc.vector.tensor_tensor(
                    out=dz_grouped[:, pair * width : (pair + 1) * width].rearrange(
                        "p (a q u e) -> p a q u e", a=2, u=2, e=2
                    ),
                    in0=banks[pair][:]
                    .rearrange("p u a q -> p u (a q)")
                    .bitcast(BF16)
                    .rearrange("p u (a q e) -> p a q u e", a=2, e=2),
                    in1=g_pair.rearrange("p a (q u e) -> p a q u e", u=2, e=2),
                    op=ALU.mult,
                )
            dz_codes = work.tile([P, HALF_TYPES * P], U32, align_bytes=64, name="dz_codes")
            dz_scales = work.tile([P, HALF_TYPES * P], U8, align_bytes=64, name="dz_scales")
            nc.vector.quantize_mx(out=dz_codes[:].bitcast(E5M2_X4), scales=dz_scales[:], in_=dz_grouped[:])
            return dz_codes, dz_scales

        def matmul_and_store(c, dz_codes, dz_scales):
            first = (c // STRIDE) * HALF_TYPES
            result = out_pool.tile([P, HALF_TYPES, ROWS], F32, name="result")
            for al in range(HALF_TYPES):
                acc = psum_mx.tile([P, ROWS], F32, name="acc")
                nc.tensor.matmul_mx(
                    out=acc[:],
                    lhsT=dz_codes[:, al * P : (al + 1) * P].bitcast(E5M2_X4),
                    lhsT_scale=dz_scales[:, al * P : (al + 1) * P],
                    rhs=w_codes[:, first + al, :].bitcast(E4M3_X4),
                    rhs_scale=w_scales[:, first + al, :],
                    start=True,
                    stop=True,
                )
                rows_out = result[:, al, :].rearrange("q (h l) -> q h l", l=W_LOW)
                rows_in = acc[:].rearrange("q (l h) -> q h l", l=W_LOW)
                if c == CHUNKS - 1 and al % 2 == 1:
                    nc.vector.tensor_copy(out=rows_out, in_=rows_in)
                else:
                    nc.scalar.copy(out=rows_out, in_=rows_in)
                if c == CHUNKS - 1 and al % 2 == 1:
                    queue = nc.sync if al == 1 else nc.scalar
                    queue.dma_start(
                        out=out_view[:, c % STRIDE, first + al - 1 : first + al + 1, :], in_=result[:, al - 1 : al + 1, :]
                    )
            if c < CHUNKS - 1:
                queue = nc.scalar if c in (4, 6) else nc.sync
                queue.dma_start(out=out_view[:, c % STRIDE, first : first + HALF_TYPES, :], in_=result[:])

        banks_of = {}
        for c in range(CHUNKS + 1):
            if c < CHUNKS:
                banks_of[c] = mask_and_transpose(c)
                if c < TYPES // 2:
                    prepare_weights(c)
            if c >= 1:
                dz_codes, dz_scales = multiply_and_quantise(c - 1, banks_of[c - 1])
                matmul_and_store(c - 1, dz_codes, dz_scales)
